import numpy as np
import ml_dtypes


def mxq(x, axis, fmt="e4m3"):
    dtype, down = {"e4m3": (ml_dtypes.float8_e4m3fn, 7), "e5m2": (ml_dtypes.float8_e5m2, 14)}[fmt]
    v = np.moveaxis(np.asarray(x, np.float32).astype(ml_dtypes.bfloat16).astype(np.float64), axis, -1)
    blocks = v.reshape(v.shape[:-1] + (-1, 32))
    amax = np.abs(blocks).max(-1, keepdims=True)
    byte = np.maximum(np.where(amax > 0, np.frexp(amax)[1] - 1 + 127, 0) - down, 1)
    scale = np.exp2(byte - 127.0)
    codes = (blocks / scale).astype(np.float32).astype(dtype).astype(np.float64)
    return np.moveaxis((codes * scale).reshape(v.shape), -1, axis)


WIDE = False


def mx_kscale(k):
    if not WIDE:
        return np.ones(k)
    levels = np.array([10, -10, 5, -5, 0])
    a = np.random.permutation(np.resize(levels, k // 512 * 4)).reshape(k // 512, 4)
    idx = np.arange(k)
    return np.exp2(a[idx // 512, idx % 128 // 32])


BF16 = ml_dtypes.bfloat16


def bf(x):
    return np.asarray(x, np.float32).astype(BF16)


def f64(x):
    return np.asarray(x).astype(np.float64)


E2M1 = np.array([0.0, 0.5, 1.0, 1.5, 2.0, 3.0, 4.0, 6.0, -0.0, -0.5, -1.0, -1.5, -2.0, -3.0, -4.0, -6.0])


def pack_weight(w, fmt):
    k, n = w.shape
    w = f64(bf(w)).reshape(k // 32, 32, n)
    amax = np.abs(w).max(1)
    if fmt == "e4m3":
        byte = np.frexp(amax)[1] - 1 + 127 - 7
    else:
        mant, ex = np.frexp(amax / 6.0)
        byte = np.where(mant > 0.5, ex, ex - 1) + 127
    byte = np.clip(np.where(amax > 0, byte, 1), 1, 254)
    scaled = (w * np.exp2(127.0 - byte)[:, None, :]).reshape(k, n).astype(np.float32)
    by_word = np.ascontiguousarray(scaled.reshape(k // 512, 128, 4, n).transpose(0, 1, 3, 2))
    if fmt == "e4m3":
        words = by_word.astype(ml_dtypes.float8_e4m3fn).view(np.uint8)
    else:
        c = by_word.astype(ml_dtypes.float4_e2m1fn).view(np.uint8) & 0xF
        words = c[..., 0::2] | (c[..., 1::2] << 4)
    return np.ascontiguousarray(words), np.ascontiguousarray(byte.astype(np.uint8).reshape(k // 512, 16, n))


def unpack_weight(words, scales, fmt):
    g, p, n, _ = words.shape
    if fmt == "e4m3":
        vals = np.ascontiguousarray(words).view(ml_dtypes.float8_e4m3fn).astype(np.float64)
    else:
        nib = np.empty((g, p, n, 4), np.uint8)
        nib[..., 0::2] = words & 0xF
        nib[..., 1::2] = words >> 4
        vals = E2M1[nib]
    vals = vals * np.repeat(np.exp2(scales.astype(np.float64) - 127.0), 8, axis=1)[..., None]
    return vals.transpose(0, 1, 3, 2).reshape(g * 512, n)

def pack4(w):
    words, scales = pack_weight(w, "e2m1")
    return words.reshape(words.shape[0], 128, -1), scales


def unpack4(words, scales):
    return unpack_weight(words.reshape(words.shape[0], 128, -1, 2), scales, "e2m1")


B, S, D_IN, D_OUT = 3, 512, 1024, 1024


def relative_shift(x):
    b, s, d = x.shape
    padded = np.concatenate([np.zeros((b, 1, d)), x], axis=1).reshape(s + 1, b, d)
    return padded[1:].reshape(b, s, d)


def setup_inputs():
    s = mx_kscale(D_IN)
    pos_embed = bf(np.random.standard_normal((B, S, D_IN)) * s)
    w = np.random.standard_normal((D_OUT, D_IN)) * 1.2 / np.sqrt(D_IN) / s[None, :]
    words, scales = pack4(np.ascontiguousarray(w.T))
    b_r = bf(np.random.standard_normal(D_OUT) * 0.3)
    return {"pos_embed": pos_embed,
            "W_r_words": words,
            "W_r_scales": scales,
            "b_r": b_r}


def reference(pos_embed, W_r_words, W_r_scales, b_r):
    shifted = relative_shift(f64(pos_embed))
    return (mxq(shifted, 2, "e4m3") @ unpack4(W_r_words, W_r_scales)) + f64(b_r)

@@ -1,0 +1,187 @@
+from contextlib import ExitStack
+
+import concourse.mybir as mybir
+from concourse.masks import make_identity
+
+F32 = mybir.dt.float32
+BF16 = mybir.dt.bfloat16
+I32 = mybir.dt.int32
+U32 = mybir.dt.uint32
+U8 = mybir.dt.uint8
+FP8X4 = mybir.dt.float8_e4m3fn_x4
+FP4X4 = mybir.dt.float4_e2m1fn_x4
+
+BATCH, SEQ, D_IN, D_OUT = 3, 512, 1024, 1024
+ROWS = BATCH * SEQ
+P = 128
+PACK = 4
+K_PASS = P * PACK
+PASSES = D_IN // K_PASS
+WORDS_PER_PASS = K_PASS // 2
+BANK = 512
+BANKS_PER_TILE = D_OUT // BANK
+ROW_TILES = ROWS // P
+TILES_PER_ROUND = 2
+ROUNDS = ROW_TILES // TILES_PER_ROUND
+PSUM_BANKS = 8
+
+FLOPS = 2 * ROWS * D_IN * D_OUT
+
+
+def source_row(r):
+    batch, place = divmod(r + BATCH, SEQ + 1)
+    return None if place == 0 else batch * SEQ + place - 1
+
+
+def selection_runs(first_row):
+    first_source = source_row(first_row)
+    runs = []
+    for column in range(P):
+        source = source_row(first_row + column)
+        if source is None:
+            continue
+        partition = source - first_source
+        if runs and runs[-1][0] + runs[-1][2] == column and runs[-1][1] + runs[-1][2] == partition:
+            runs[-1][2] += 1
+        else:
+            runs.append([column, partition, 1])
+    return first_source, runs
+
+
+def tile_relativemultiheadattention_pa_kernel(tc, pos_embed, W_r_words, W_r_scales, b_r, out):
+    nc = tc.nc
+    x_rows = pos_embed.flatten_outer_dims()
+    out_rows = out.flatten_outer_dims()
+
+    with ExitStack() as ctx:
+        ctx.enter_context(tc.manual_schedule())
+        const = ctx.enter_context(tc.tile_pool(name="const", bufs=1))
+        x_pool = ctx.enter_context(tc.tile_pool(name="x", bufs=ROW_TILES))
+        mx_pool = ctx.enter_context(tc.tile_pool(name="mx", bufs=2 * TILES_PER_ROUND))
+        y_pool = ctx.enter_context(tc.tile_pool(name="y", bufs=2 * TILES_PER_ROUND))
+        xt_pool = ctx.enter_context(tc.psum_pool(name="xt", bufs=TILES_PER_ROUND))
+        acc_pool = ctx.enter_context(tc.psum_pool(name="acc", bufs=PSUM_BANKS - TILES_PER_ROUND))
+
+        w_scales = const.tile([P, PASSES, D_OUT], U8, align_bytes=64)
+        nc.vector.memset(w_scales[:].bitcast(I32), 0)
+        bias_row = const.tile([P, D_OUT], BF16)
+        nc.vector.memset(bias_row[:], 0.0)
+        ones = const.tile([P, P], BF16)
+        nc.vector.memset(ones[:], 1.0)
+        identity = const.tile([P, P], F32)
+        make_identity(nc, identity[:])
+
+        first_sources = []
+        selections = []
+        for i in range(ROW_TILES):
+            first_source, runs = selection_runs(P * i)
+            first_sources.append(first_source)
+            if runs == [[0, 0, P]]:
+                selections.append(identity)
+                continue
+            selection = const.tile([P, P], F32, name="selection%d" % i)
+            nc.vector.memset(selection[:], 0.0)
+            for column, partition, length in runs:
+                nc.vector.tensor_copy(
+                    out=selection[:, column : column + length], in_=identity[:, partition : partition + length]
+                )
+            selections.append(selection)
+
+        x_tiles = []
+
+        def load_rows(i):
+            x_tile = x_pool.tile([P, D_IN], BF16)
+            nc.sync.dma_start(out=x_tile[:], in_=x_rows[first_sources[i] : first_sources[i] + P, :])
+            x_tiles.append(x_tile)
+
+        for i in range(TILES_PER_ROUND):
+            load_rows(i)
+        nc.scalar.dma_start(out=bias_row[0:1, :], in_=b_r.unsqueeze(0))
+        for quadrant in range(4):
+            nc.sync.dma_start(
+                out=w_scales[32 * quadrant : 32 * quadrant + 4, :, :].bitcast(I32),
+                in_=W_r_scales[:, 4 * quadrant : 4 * quadrant + 4, :].rearrange("g r n -> r g n").bitcast(I32),
+            )
+        w_words = const.tile([P, PASSES, 2 * D_OUT], U8, align_bytes=64)
+        nc.sync.dma_start(out=w_words[:].bitcast(I32), in_=W_r_words.rearrange("g p b -> p g b").bitcast(I32))
+        for i in range(TILES_PER_ROUND, ROW_TILES):
+            load_rows(i)
+
+        grouped_tiles = {}
+        code_tiles = {}
+        acc_tiles = {}
+
+        def transpose_tile(i):
+            x_words = x_tiles[i][:].bitcast(F32)
+            xt = xt_pool.tile([P, PASSES, 2, P], F32)
+            for g in range(PASSES):
+                for u in range(2):
+                    nc.tensor.transpose(
+                        xt[:, g, u, :],
+                        x_words[:, WORDS_PER_PASS * g + u : WORDS_PER_PASS * (g + 1) : 2],
+                        selections[i][:],
+                    )
+            grouped = mx_pool.tile([P, PASSES * P * PACK], BF16, align_bytes=64)
+            nc.scalar.copy(
+                out=grouped[:].bitcast(F32).rearrange("p (g r u) -> p g r u", g=PASSES, u=2),
+                in_=xt[:].rearrange("p g u r -> p g r u"),
+            )
+            grouped_tiles[i] = grouped
+
+        def quantise_tile(i):
+            codes = mx_pool.tile([P, PASSES, P], U32, align_bytes=64)
+            scales = mx_pool.tile([P, PASSES, P], U8, align_bytes=64)
+            nc.vector.quantize_mx(
+                out=codes[:].rearrange("p g r -> p (g r)").bitcast(FP8X4),
+                scales=scales[:].rearrange("p g r -> p (g r)"),
+                in_=grouped_tiles[i][:],
+            )
+            code_tiles[i] = (codes, scales)
+
+        def multiply_tile(i):
+            codes, scales = code_tiles[i]
+            for h in range(BANKS_PER_TILE):
+                acc = acc_pool.tile([P, BANK], F32)
+                for g in range(PASSES):
+                    nc.tensor.matmul_mx(
+                        out=acc[:],
+                        lhsT=codes[:, g, :].bitcast(FP8X4),
+                        lhsT_scale=scales[:, g, :],
+                        rhs=w_words[:, g, 2 * BANK * h : 2 * BANK * (h + 1)].bitcast(FP4X4),
+                        rhs_scale=w_scales[:, g, BANK * h : BANK * (h + 1)],
+                        start=(g == 0),
+                        stop=(g == PASSES - 1),
+                    )
+                acc_tiles[i, h] = acc
+
+        def finish_tile(i):
+            y = y_pool.tile([P, D_OUT], F32)
+            for h in range(BANKS_PER_TILE):
+                columns = slice(BANK * h, BANK * (h + 1))
+                nc.vector.tensor_add(out=y[:, columns], in0=acc_tiles[i, h][:], in1=bias[:, columns])
+            nc.sync.dma_start(out=out_rows[P * i : P * (i + 1), :], in_=y[:])
+
+        def tiles_of(r):
+            return range(TILES_PER_ROUND * r, TILES_PER_ROUND * (r + 1))
+
+        for i in tiles_of(0):
+            transpose_tile(i)
+        bias = const.tile([P, D_OUT], F32)
+        for h in range(BANKS_PER_TILE):
+            columns = slice(BANK * h, BANK * (h + 1))
+            spread = acc_pool.tile([P, BANK], F32, tag="acc")
+            nc.tensor.matmul(out=spread[:], lhsT=ones[:], rhs=bias_row[:, columns], start=True, stop=True)
+            nc.scalar.copy(out=bias[:, columns], in_=spread[:])
+        for i in tiles_of(0):
+            quantise_tile(i)
+        for r in range(ROUNDS):
+            if r + 1 < ROUNDS:
+                for i in tiles_of(r + 1):
+                    transpose_tile(i)
+            for i in tiles_of(r):
+                multiply_tile(i)
+            if r + 1 < ROUNDS:
+                for i in tiles_of(r + 1):
+                    quantise_tile(i)
+            for i in tiles_of(r):
+                finish_tile(i)

@@ -23,6 +23,7 @@ BANKS_PER_TILE = D_OUT // BANK
 ROW_TILES = ROWS // P
 TILES_PER_ROUND = 2
 ROUNDS = ROW_TILES // TILES_PER_ROUND
+SORT_AHEAD = 2
 PSUM_BANKS = 8
 
 FLOPS = 2 * ROWS * D_IN * D_OUT
@@ -57,6 +58,7 @@ def tile_relativemultiheadattention_pa_kernel(tc, pos_embed, W_r_words, W_r_scal
         ctx.enter_context(tc.manual_schedule())
         const = ctx.enter_context(tc.tile_pool(name="const", bufs=1))
         x_pool = ctx.enter_context(tc.tile_pool(name="x", bufs=ROW_TILES))
+        sorted_pool = ctx.enter_context(tc.tile_pool(name="sorted", bufs=2 * TILES_PER_ROUND))
         mx_pool = ctx.enter_context(tc.tile_pool(name="mx", bufs=2 * TILES_PER_ROUND))
         y_pool = ctx.enter_context(tc.tile_pool(name="y", bufs=2 * TILES_PER_ROUND))
         xt_pool = ctx.enter_context(tc.psum_pool(name="xt", bufs=TILES_PER_ROUND))
@@ -107,20 +109,29 @@ def tile_relativemultiheadattention_pa_kernel(tc, pos_embed, W_r_words, W_r_scal
         for i in range(TILES_PER_ROUND, ROW_TILES):
             load_rows(i)
 
+        sorted_tiles = {}
         grouped_tiles = {}
         code_tiles = {}
         acc_tiles = {}
+
+        def sort_tile(i):
+            x_sorted = sorted_pool.tile([P, PASSES, 2, P], F32)
+            nc.scalar.copy(
+                out=x_sorted[:],
+                in_=x_tiles[i][:].bitcast(F32).rearrange("r (g p u) -> r g u p", g=PASSES, u=2),
+            )
+            sorted_tiles[i] = x_sorted
 
         def transpose_tile(i):
             x_words = x_tiles[i][:].bitcast(F32)
             xt = xt_pool.tile([P, PASSES, 2, P], F32)
             for g in range(PASSES):
                 for u in range(2):
-                    nc.tensor.transpose(
-                        xt[:, g, u, :],
-                        x_words[:, WORDS_PER_PASS * g + u : WORDS_PER_PASS * (g + 1) : 2],
-                        selections[i][:],
-                    )
+                    if i in sorted_tiles:
+                        words = sorted_tiles[i][:, g, u, :]
+                    else:
+                        words = x_words[:, WORDS_PER_PASS * g + u : WORDS_PER_PASS * (g + 1) : 2]
+                    nc.tensor.transpose(xt[:, g, u, :], words, selections[i][:])
             grouped = mx_pool.tile([P, PASSES * P * PACK], BF16, align_bytes=64)
             nc.scalar.copy(
                 out=grouped[:].bitcast(F32).rearrange("p (g r u) -> p g r u", g=PASSES, u=2),
@@ -178,6 +189,9 @@ def tile_relativemultiheadattention_pa_kernel(tc, pos_embed, W_r_words, W_r_scal
             if r + 1 < ROUNDS:
                 for i in tiles_of(r + 1):
                     transpose_tile(i)
+            if r + SORT_AHEAD < ROUNDS:
+                for i in tiles_of(r + SORT_AHEAD):
+                    sort_tile(i)
             for i in tiles_of(r):
                 multiply_tile(i)
             if r + 1 < ROUNDS:

@@ -60,7 +60,7 @@ def tile_relativemultiheadattention_pa_kernel(tc, pos_embed, W_r_words, W_r_scal
         x_pool = ctx.enter_context(tc.tile_pool(name="x", bufs=ROW_TILES))
         sorted_pool = ctx.enter_context(tc.tile_pool(name="sorted", bufs=2 * TILES_PER_ROUND))
         mx_pool = ctx.enter_context(tc.tile_pool(name="mx", bufs=2 * TILES_PER_ROUND))
-        y_pool = ctx.enter_context(tc.tile_pool(name="y", bufs=2 * TILES_PER_ROUND))
+        y_pool = ctx.enter_context(tc.tile_pool(name="y", bufs=ROW_TILES))
         xt_pool = ctx.enter_context(tc.psum_pool(name="xt", bufs=TILES_PER_ROUND))
         acc_pool = ctx.enter_context(tc.psum_pool(name="acc", bufs=PSUM_BANKS - TILES_PER_ROUND))
 

@@ -64,7 +64,7 @@ def tile_relativemultiheadattention_pa_kernel(tc, pos_embed, W_r_words, W_r_scal
         xt_pool = ctx.enter_context(tc.psum_pool(name="xt", bufs=TILES_PER_ROUND))
         acc_pool = ctx.enter_context(tc.psum_pool(name="acc", bufs=PSUM_BANKS - TILES_PER_ROUND))
 
-        w_scales = const.tile([P, PASSES, D_OUT], U8, align_bytes=64)
+        w_scales = const.tile([P, PASSES, D_OUT], U8, align_bytes=256)
         nc.vector.memset(w_scales[:].bitcast(I32), 0)
         bias_row = const.tile([P, D_OUT], BF16)
         nc.vector.memset(bias_row[:], 0.0)
@@ -104,7 +104,7 @@ def tile_relativemultiheadattention_pa_kernel(tc, pos_embed, W_r_words, W_r_scal
                 out=w_scales[32 * quadrant : 32 * quadrant + 4, :, :].bitcast(I32),
                 in_=W_r_scales[:, 4 * quadrant : 4 * quadrant + 4, :].rearrange("g r n -> r g n").bitcast(I32),
             )
-        w_words = const.tile([P, PASSES, 2 * D_OUT], U8, align_bytes=64)
+        w_words = const.tile([P, PASSES, 2 * D_OUT], U8, align_bytes=256)
         nc.sync.dma_start(out=w_words[:].bitcast(I32), in_=W_r_words.rearrange("g p b -> p g b").bitcast(I32))
         for i in range(TILES_PER_ROUND, ROW_TILES):
             load_rows(i)
@@ -132,7 +132,7 @@ def tile_relativemultiheadattention_pa_kernel(tc, pos_embed, W_r_words, W_r_scal
                     else:
                         words = x_words[:, WORDS_PER_PASS * g + u : WORDS_PER_PASS * (g + 1) : 2]
                     nc.tensor.transpose(xt[:, g, u, :], words, selections[i][:])
-            grouped = mx_pool.tile([P, PASSES * P * PACK], BF16, align_bytes=64)
+            grouped = mx_pool.tile([P, PASSES * P * PACK], BF16, align_bytes=256)
             nc.scalar.copy(
                 out=grouped[:].bitcast(F32).rearrange("p (g r u) -> p g r u", g=PASSES, u=2),
                 in_=xt[:].rearrange("p g u r -> p g r u"),
@@ -140,8 +140,8 @@ def tile_relativemultiheadattention_pa_kernel(tc, pos_embed, W_r_words, W_r_scal
             grouped_tiles[i] = grouped
 
         def quantise_tile(i):
-            codes = mx_pool.tile([P, PASSES, P], U32, align_bytes=64)
-            scales = mx_pool.tile([P, PASSES, P], U8, align_bytes=64)
+            codes = mx_pool.tile([P, PASSES, P], U32, align_bytes=256)
+            scales = mx_pool.tile([P, PASSES, P], U8, align_bytes=256)
             nc.vector.quantize_mx(
                 out=codes[:].rearrange("p g r -> p (g r)").bitcast(FP8X4),
                 scales=scales[:].rearrange("p g r -> p (g r)"),

from contextlib import ExitStack

import concourse.mybir as mybir
from concourse.masks import make_identity

F32 = mybir.dt.float32
BF16 = mybir.dt.bfloat16
I32 = mybir.dt.int32
U32 = mybir.dt.uint32
U8 = mybir.dt.uint8
FP8X4 = mybir.dt.float8_e4m3fn_x4
FP4X4 = mybir.dt.float4_e2m1fn_x4

BATCH, SEQ, D_IN, D_OUT = 3, 512, 1024, 1024
ROWS = BATCH * SEQ
P = 128
PACK = 4
K_PASS = P * PACK
PASSES = D_IN // K_PASS
WORDS_PER_PASS = K_PASS // 2
BANK = 512
BANKS_PER_TILE = D_OUT // BANK
ROW_TILES = ROWS // P
TILES_PER_ROUND = 2
ROUNDS = ROW_TILES // TILES_PER_ROUND
SORT_AHEAD = 2
PSUM_BANKS = 8

FLOPS = 2 * ROWS * D_IN * D_OUT


def source_row(r):
    batch, place = divmod(r + BATCH, SEQ + 1)
    return None if place == 0 else batch * SEQ + place - 1


def selection_runs(first_row):
    first_source = source_row(first_row)
    runs = []
    for column in range(P):
        source = source_row(first_row + column)
        if source is None:
            continue
        partition = source - first_source
        if runs and runs[-1][0] + runs[-1][2] == column and runs[-1][1] + runs[-1][2] == partition:
            runs[-1][2] += 1
        else:
            runs.append([column, partition, 1])
    return first_source, runs


def tile_relativemultiheadattention_pa_kernel(tc, pos_embed, W_r_words, W_r_scales, b_r, out):
    nc = tc.nc
    x_rows = pos_embed.flatten_outer_dims()
    out_rows = out.flatten_outer_dims()

    with ExitStack() as ctx:
        ctx.enter_context(tc.manual_schedule())
        const = ctx.enter_context(tc.tile_pool(name="const", bufs=1))
        x_pool = ctx.enter_context(tc.tile_pool(name="x", bufs=ROW_TILES))
        sorted_pool = ctx.enter_context(tc.tile_pool(name="sorted", bufs=2 * TILES_PER_ROUND))
        mx_pool = ctx.enter_context(tc.tile_pool(name="mx", bufs=2 * TILES_PER_ROUND))
        y_pool = ctx.enter_context(tc.tile_pool(name="y", bufs=ROW_TILES))
        xt_pool = ctx.enter_context(tc.psum_pool(name="xt", bufs=TILES_PER_ROUND))
        acc_pool = ctx.enter_context(tc.psum_pool(name="acc", bufs=PSUM_BANKS - TILES_PER_ROUND))

        w_scales = const.tile([P, PASSES, D_OUT], U8, align_bytes=256)
        nc.vector.memset(w_scales[:].bitcast(I32), 0)
        bias_row = const.tile([P, D_OUT], BF16)
        nc.vector.memset(bias_row[:], 0.0)
        ones = const.tile([P, P], BF16)
        nc.vector.memset(ones[:], 1.0)
        identity = const.tile([P, P], F32)
        make_identity(nc, identity[:])

        first_sources = []
        selections = []
        for i in range(ROW_TILES):
            first_source, runs = selection_runs(P * i)
            first_sources.append(first_source)
            if runs == [[0, 0, P]]:
                selections.append(identity)
                continue
            selection = const.tile([P, P], F32, name="selection%d" % i)
            nc.vector.memset(selection[:], 0.0)
            for column, partition, length in runs:
                nc.vector.tensor_copy(
                    out=selection[:, column : column + length], in_=identity[:, partition : partition + length]
                )
            selections.append(selection)

        x_tiles = []

        def load_rows(i):
            x_tile = x_pool.tile([P, D_IN], BF16)
            nc.sync.dma_start(out=x_tile[:], in_=x_rows[first_sources[i] : first_sources[i] + P, :])
            x_tiles.append(x_tile)

        for i in range(TILES_PER_ROUND):
            load_rows(i)
        nc.scalar.dma_start(out=bias_row[0:1, :], in_=b_r.unsqueeze(0))
        for quadrant in range(4):
            nc.sync.dma_start(
                out=w_scales[32 * quadrant : 32 * quadrant + 4, :, :].bitcast(I32),
                in_=W_r_scales[:, 4 * quadrant : 4 * quadrant + 4, :].rearrange("g r n -> r g n").bitcast(I32),
            )
        w_words = const.tile([P, PASSES, 2 * D_OUT], U8, align_bytes=256)
        nc.sync.dma_start(out=w_words[:].bitcast(I32), in_=W_r_words.rearrange("g p b -> p g b").bitcast(I32))
        for i in range(TILES_PER_ROUND, ROW_TILES):
            load_rows(i)

        sorted_tiles = {}
        grouped_tiles = {}
        code_tiles = {}
        acc_tiles = {}

        def sort_tile(i):
            x_sorted = sorted_pool.tile([P, PASSES, 2, P], F32)
            nc.scalar.copy(
                out=x_sorted[:],
                in_=x_tiles[i][:].bitcast(F32).rearrange("r (g p u) -> r g u p", g=PASSES, u=2),
            )
            sorted_tiles[i] = x_sorted

        def transpose_tile(i):
            x_words = x_tiles[i][:].bitcast(F32)
            xt = xt_pool.tile([P, PASSES, 2, P], F32)
            for g in range(PASSES):
                for u in range(2):
                    if i in sorted_tiles:
                        words = sorted_tiles[i][:, g, u, :]
                    else:
                        words = x_words[:, WORDS_PER_PASS * g + u : WORDS_PER_PASS * (g + 1) : 2]
                    nc.tensor.transpose(xt[:, g, u, :], words, selections[i][:])
            grouped = mx_pool.tile([P, PASSES * P * PACK], BF16, align_bytes=256)
            nc.scalar.copy(
                out=grouped[:].bitcast(F32).rearrange("p (g r u) -> p g r u", g=PASSES, u=2),
                in_=xt[:].rearrange("p g u r -> p g r u"),
            )
            grouped_tiles[i] = grouped

        def quantise_tile(i):
            codes = mx_pool.tile([P, PASSES, P], U32, align_bytes=256)
            scales = mx_pool.tile([P, PASSES, P], U8, align_bytes=256)
            nc.vector.quantize_mx(
                out=codes[:].rearrange("p g r -> p (g r)").bitcast(FP8X4),
                scales=scales[:].rearrange("p g r -> p (g r)"),
                in_=grouped_tiles[i][:],
            )
            code_tiles[i] = (codes, scales)

        def multiply_tile(i):
            codes, scales = code_tiles[i]
            for h in range(BANKS_PER_TILE):
                acc = acc_pool.tile([P, BANK], F32)
                for g in range(PASSES):
                    nc.tensor.matmul_mx(
                        out=acc[:],
                        lhsT=codes[:, g, :].bitcast(FP8X4),
                        lhsT_scale=scales[:, g, :],
                        rhs=w_words[:, g, 2 * BANK * h : 2 * BANK * (h + 1)].bitcast(FP4X4),
                        rhs_scale=w_scales[:, g, BANK * h : BANK * (h + 1)],
                        start=(g == 0),
                        stop=(g == PASSES - 1),
                    )
                acc_tiles[i, h] = acc

        def finish_tile(i):
            y = y_pool.tile([P, D_OUT], F32)
            for h in range(BANKS_PER_TILE):
                columns = slice(BANK * h, BANK * (h + 1))
                nc.vector.tensor_add(out=y[:, columns], in0=acc_tiles[i, h][:], in1=bias[:, columns])
            nc.sync.dma_start(out=out_rows[P * i : P * (i + 1), :], in_=y[:])

        def tiles_of(r):
            return range(TILES_PER_ROUND * r, TILES_PER_ROUND * (r + 1))

        for i in tiles_of(0):
            transpose_tile(i)
        bias = const.tile([P, D_OUT], F32)
        for h in range(BANKS_PER_TILE):
            columns = slice(BANK * h, BANK * (h + 1))
            spread = acc_pool.tile([P, BANK], F32, tag="acc")
            nc.tensor.matmul(out=spread[:], lhsT=ones[:], rhs=bias_row[:, columns], start=True, stop=True)
            nc.scalar.copy(out=bias[:, columns], in_=spread[:])
        for i in tiles_of(0):
            quantise_tile(i)
        for r in range(ROUNDS):
            if r + 1 < ROUNDS:
                for i in tiles_of(r + 1):
                    transpose_tile(i)
            if r + SORT_AHEAD < ROUNDS:
                for i in tiles_of(r + SORT_AHEAD):
                    sort_tile(i)
            for i in tiles_of(r):
                multiply_tile(i)
            if r + 1 < ROUNDS:
                for i in tiles_of(r + 1):
                    quantise_tile(i)
            for i in tiles_of(r):
                finish_tile(i)
